import numpy as np
import ml_dtypes


def mxq(x, axis, fmt="e4m3"):
    dtype, down = {"e4m3": (ml_dtypes.float8_e4m3fn, 7), "e5m2": (ml_dtypes.float8_e5m2, 14)}[fmt]
    v = np.moveaxis(np.asarray(x, np.float32).astype(ml_dtypes.bfloat16).astype(np.float64), axis, -1)
    blocks = v.reshape(v.shape[:-1] + (-1, 32))
    amax = np.abs(blocks).max(-1, keepdims=True)
    byte = np.maximum(np.where(amax > 0, np.frexp(amax)[1] - 1 + 127, 0) - down, 1)
    scale = np.exp2(byte - 127.0)
    codes = (blocks / scale).astype(np.float32).astype(dtype).astype(np.float64)
    return np.moveaxis((codes * scale).reshape(v.shape), -1, axis)


WIDE = False


def mx_kscale(k):
    if not WIDE:
        return np.ones(k)
    levels = np.array([10, -10, 5, -5, 0])
    a = np.random.permutation(np.resize(levels, k // 512 * 4)).reshape(k // 512, 4)
    idx = np.arange(k)
    return np.exp2(a[idx // 512, idx % 128 // 32])


BF16 = ml_dtypes.bfloat16


def bf(x):
    return np.asarray(x, np.float32).astype(BF16)


def f64(x):
    return np.asarray(x).astype(np.float64)


B, I, H = 512, 1024, 1024
QH = H % 512 == 0


def sigmoid(v):
    return 1.0 / (1.0 + np.exp(-v))


def setup_inputs():
    s = mx_kscale(I)
    t = mx_kscale(H) if QH else np.ones(H)
    n = np.random.standard_normal
    aw, ar = 0.6 / np.sqrt(I), 0.6 / np.sqrt(H)
    return {"xt": bf(n((B, I)) * s), "cx": bf(n((B, H))), "hx": bf(n((B, H)) * t),
            "w_fg": bf(n((H, I)) * aw / s), "w_ig": bf(n((H, I)) * aw / s), "w_og": bf(n((H, I)) * aw / s), "w_ci": bf(n((H, I)) * aw / s),
            "r_fg": bf(n((H, H)) * ar / t), "r_ig": bf(n((H, H)) * ar / t), "r_og": bf(n((H, H)) * ar / t), "r_ci": bf(n((H, H)) * ar / t),
            "b_fg": bf(n(H) * 0.3), "b_ig": bf(n(H) * 0.3), "b_og": bf(n(H) * 0.3), "b_ci": bf(n(H) * 0.3)}


def reference(xt, cx, hx, w_fg, w_ig, w_og, w_ci, r_fg, r_ig, r_og, r_ci, b_fg, b_ig, b_og, b_ci):
    W = np.concatenate([f64(w_fg), f64(w_ig), f64(w_og), f64(w_ci)], axis=0)
    R = np.concatenate([f64(r_fg), f64(r_ig), f64(r_og), f64(r_ci)], axis=0)
    b = np.concatenate([f64(b_fg), f64(b_ig), f64(b_og), f64(b_ci)], axis=0)
    gx = mxq(f64(xt), 1, "e4m3") @ mxq(W, 1, "e4m3").T
    if QH:
        gh = mxq(f64(hx), 1, "e4m3") @ mxq(R, 1, "e4m3").T
    else:
        gh = f64(hx) @ R.T
    gates = gx + gh + b
    f, i, o, g = np.split(gates, 4, axis=-1)
    ft = sigmoid(f)
    it = sigmoid(i)
    ot = sigmoid(o)
    ct = ft * f64(cx) + it * np.tanh(g)
    ht = ot * np.tanh(ct)
    return (ht, ct)

@@ -1,0 +1,365 @@
+from contextlib import ExitStack
+
+import concourse.mybir as mybir
+from concourse.masks import make_identity
+
+F32 = mybir.dt.float32
+BF16 = mybir.dt.bfloat16
+U32 = mybir.dt.uint32
+U8 = mybir.dt.uint8
+I32 = mybir.dt.int32
+FP8X4 = mybir.dt.float8_e4m3fn_x4
+ACT = mybir.ActivationFunctionType
+ALU = mybir.AluOpType
+
+P = 128
+B, I, H = 512, 1024, 1024
+NCH = H // P
+ALL = (0, 1, 2, 3)
+FLOPS = 2 * B * (4 * H) * (I + H)
+
+CFG = {"cx_after": 3, "nru": 7, "vshare": (), "g_ops": (), "pin": True}
+
+
+def tile_lstmcell_kernel(tc, xt, cx, hx, w_fg, w_ig, w_og, w_ci, r_fg, r_ig, r_og, r_ci,
+                                    b_fg, b_ig, b_og, b_ci, out_0, out_1):
+    nc = tc.nc
+    cfg = CFG
+    with ExitStack() as ctx:
+        if cfg["pin"]:
+            ctx.enter_context(tc.manual_schedule())
+        const = ctx.enter_context(tc.tile_pool(name="const", bufs=1))
+        raw_pool = ctx.enter_context(tc.tile_pool(name="raw", bufs=4 * cfg["nru"]))
+        grp_pool = ctx.enter_context(tc.tile_pool(name="grp", bufs=3))
+        wc_pool = ctx.enter_context(tc.tile_pool(name="wc", bufs=4))
+        pre_pool = ctx.enter_context(tc.tile_pool(name="pre", bufs=4))
+        psum = ctx.enter_context(tc.psum_pool(name="ps", bufs=1))
+
+        w_in = (w_fg, w_ig, w_og, w_ci)
+        r_in = (r_fg, r_ig, r_og, r_ci)
+        b_in = (b_fg, b_ig, b_og, b_ci)
+        xt_v = xt.rearrange("(m j) k -> m j k", j=4)
+        hx_v = hx.rearrange("(m j) k -> m j k", j=4)
+        cx_v = cx.rearrange("(m j) h -> m j h", j=4)
+        ht_v = out_0.rearrange("(m j) h -> m j h", j=4)
+        ct_v = out_1.rearrange("(m j) h -> m j h", j=4)
+
+        ident = const.tile([P, P], F32, name="ident")
+        ones = const.tile([P, P], BF16, name="ones")
+        zrow = const.tile([P, 4 * H], BF16, name="zrow")
+        bias_bc = const.tile([P, NCH, 512], BF16, name="bias_bc")
+        cx_sb = const.tile([P, 4, H], BF16, name="cx_sb")
+        ct_all = const.tile([P, 4, H], F32, name="ct_all")
+        ht_all = const.tile([P, 4, H], F32, name="ht_all")
+        warm = const.tile([P, 1], F32, name="warm")
+        warm2 = const.tile([P, 1], F32, name="warm2")
+        a_codes = [const.tile([P, 2, 512], U32, name="a_codes%d" % s, align_bytes=64) for s in range(2)]
+        a_scales = [const.tile([P, 2, 512], U8, name="a_scales%d" % s, align_bytes=64) for s in range(2)]
+
+        st = {"fill": 0, "ring": 4, "g": 0, "load": 0}
+        raws = {}
+        banks = {}
+        grps = {}
+        codes = {("X", 0): (a_codes[0], a_scales[0]), ("H", 0): (a_codes[1], a_scales[1])}
+        gates = {}
+        pres = {}
+
+        def load_bias():
+            nc.vector.memset(zrow[:].bitcast(I32), 0)
+            nc.vector.memset(warm[:], 0.0)
+            nc.vector.memset(ones[:], 1.0)
+            make_identity(nc, ident[:])
+            zv = zrow[0:1, :].rearrange("o (c q h) -> o c q h", c=NCH, q=4)
+            for q in range(4):
+                nc.scalar.dma_start(out=zv[:, :, q, :], in_=b_in[q].rearrange("(o c h) -> o c h", o=1, c=NCH))
+            nc.scalar.activation(out=warm2[:], in_=warm[:], func=ACT.Sigmoid)
+
+        def load_unit(u):
+            kind, c = u
+            tiles = []
+            for q in range(4):
+                t = raw_pool.tile([P, 1024], BF16, name="raw_%s%d_%d" % (kind, c, q), tag="raw")
+                if kind == "X":
+                    src = xt_v[:, q, :]
+                elif kind == "H":
+                    src = hx_v[:, q, :]
+                elif kind == "W":
+                    src = w_in[q][c * P:(c + 1) * P, :]
+                else:
+                    src = r_in[q][c * P:(c + 1) * P, :]
+                nc.sync.dma_start(out=t[:], in_=src)
+                tiles.append(t)
+            raws[u] = tiles
+
+        def load_cx():
+            nc.sync.dma_start(out=cx_sb[:], in_=cx_v)
+
+        def bank_for(u, i):
+            if (u, i) not in banks:
+                tag = "tb%d" % (st["fill"] % st["ring"])
+                st["fill"] += 1
+                banks[(u, i)] = psum.tile([P, 512], F32, name="tp_%s%d_%d" % (u[0], u[1], i), tag=tag)
+            return banks[(u, i)]
+
+        def tr(u, q, g, w, ps, slot):
+            col = 256 * g + 128 * w
+            nc.tensor.transpose(out=ps[:, slot * P:(slot + 1) * P], in_=raws[u][q][:].bitcast(F32)[:, col:col + P],
+                                identity=ident[:])
+
+        def fill(u, i):
+            g, pr = divmod(i, 2)
+            ps = bank_for(u, i)
+            for t in range(2):
+                for w in range(2):
+                    tr(u, 2 * pr + t, g, w, ps, 2 * t + w)
+
+        def fills_pair(u, pr):
+            for t in range(2):
+                for g in range(2):
+                    ps = bank_for(u, 2 * g + pr)
+                    for w in range(2):
+                        tr(u, 2 * pr + t, g, w, ps, 2 * t + w)
+
+        def co(u, i, eng):
+            g, pr = divmod(i, 2)
+            if u not in grps:
+                grps[u] = grp_pool.tile([P, 2, 2048], BF16, name="grp_%s%d" % u, tag="grp", align_bytes=64)
+            dst = grps[u][:, g, pr * 1024:(pr + 1) * 1024].bitcast(F32).rearrange("p (t r w) -> p t r w", t=2, w=2)
+            src = banks[(u, i)][:].rearrange("p (t w r) -> p t r w", t=2, w=2)
+            if eng == "S":
+                nc.scalar.copy(out=dst, in_=src)
+            else:
+                nc.vector.tensor_copy(out=dst, in_=src)
+
+        def quant(u, g):
+            if u not in codes:
+                codes[u] = (wc_pool.tile([P, 2, 512], U32, name="wc_%s%d" % u, tag="wc", align_bytes=64),
+                            wc_pool.tile([P, 2, 512], U8, name="ws_%s%d" % u, tag="ws", align_bytes=64))
+            cd, sc = codes[u]
+            if g is None:
+                nc.vector.quantize_mx(out=cd[:].rearrange("p g n -> p (g n)").bitcast(FP8X4),
+                                      scales=sc[:].rearrange("p g n -> p (g n)"),
+                                      in_=grps[u][:].rearrange("p g n -> p (g n)"))
+            else:
+                nc.vector.quantize_mx(out=cd[:, g, :].bitcast(FP8X4), scales=sc[:, g, :], in_=grps[u][:, g, :])
+
+        def mx(c, bt, s, g, bank=None):
+            if (c, bt) not in gates:
+                if bank is None:
+                    bank = "gb%d" % (st["g"] % 3)
+                    st["g"] += 1
+                gates[(c, bt)] = psum.tile([P, 512], F32, name="gate_%d_%d" % (c, bt), tag=bank)
+            acd, asc = codes[("XH"[s], 0)]
+            wcd, wsc = codes[("WR"[s], c)]
+            nc.tensor.matmul_mx(out=gates[(c, bt)][:],
+                                lhsT=acd[:, g, bt * P:(bt + 1) * P].bitcast(FP8X4),
+                                lhsT_scale=asc[:, g, bt * P:(bt + 1) * P],
+                                rhs=wcd[:, g, :].bitcast(FP8X4),
+                                rhs_scale=wsc[:, g, :],
+                                start=(s == 0 and g == 0), stop=(s == 1 and g == 1))
+
+        def ba(c, bt):
+            if c not in pres:
+                pres[c] = pre_pool.tile([P, 4, 512], F32, name="pre_%d" % c, tag="pre")
+            nc.vector.tensor_tensor(out=pres[c][:, bt, :], in0=gates[(c, bt)][:], in1=bias_bc[:, c, :], op=ALU.add)
+
+        def act1(c, bts):
+            b0, b1 = bts[0], bts[-1] + 1
+            nc.scalar.activation(out=pres[c][:, b0:b1, 0:384], in_=pres[c][:, b0:b1, 0:384], func=ACT.Sigmoid)
+            nc.scalar.activation(out=pres[c][:, b0:b1, 384:512], in_=pres[c][:, b0:b1, 384:512], func=ACT.Tanh)
+
+        def ew_eng(name, c):
+            return nc.gpsimd if (name, c) in cfg["g_ops"] else nc.vector
+
+        def op_a(c, bts):
+            b0, b1 = bts[0], bts[-1] + 1
+            ew_eng("a", c).tensor_tensor(out=pres[c][:, b0:b1, 0:128], in0=pres[c][:, b0:b1, 0:128],
+                                         in1=cx_sb[:, b0:b1, c * P:(c + 1) * P], op=ALU.mult)
+
+        def op_b(c, bts):
+            b0, b1 = bts[0], bts[-1] + 1
+            ew_eng("b", c).tensor_tensor(out=pres[c][:, b0:b1, 128:256], in0=pres[c][:, b0:b1, 128:256],
+                                         in1=pres[c][:, b0:b1, 384:512], op=ALU.mult)
+
+        def op_ct(c, bts):
+            b0, b1 = bts[0], bts[-1] + 1
+            ew_eng("ct", c).tensor_tensor(out=ct_all[:, b0:b1, c * P:(c + 1) * P], in0=pres[c][:, b0:b1, 0:128],
+                                          in1=pres[c][:, b0:b1, 128:256], op=ALU.add)
+
+        def act2(c, bts):
+            b0, b1 = bts[0], bts[-1] + 1
+            nc.scalar.activation(out=pres[c][:, b0:b1, 384:512], in_=ct_all[:, b0:b1, c * P:(c + 1) * P], func=ACT.Tanh)
+
+        def op_ht(c, bts):
+            b0, b1 = bts[0], bts[-1] + 1
+            ew_eng("ht", c).tensor_tensor(out=ht_all[:, b0:b1, c * P:(c + 1) * P], in0=pres[c][:, b0:b1, 256:384],
+                                          in1=pres[c][:, b0:b1, 384:512], op=ALU.mult)
+
+        def store(c0, c1, bts):
+            b0, b1 = bts[0], bts[-1] + 1
+            nc.sync.dma_start(out=ct_v[:, b0:b1, c0 * P:c1 * P], in_=ct_all[:, b0:b1, c0 * P:c1 * P])
+            nc.sync.dma_start(out=ht_v[:, b0:b1, c0 * P:c1 * P], in_=ht_all[:, b0:b1, c0 * P:c1 * P])
+
+        bias_ps = {}
+
+        def bias_mm(i, bank):
+            bias_ps[i] = psum.tile([P, 1024], BF16, name="bias_ps%d" % i, tag=bank)
+            for k in range(2):
+                nc.tensor.matmul(out=bias_ps[i][:, k * 512:(k + 1) * 512], lhsT=ones[:],
+                                 rhs=zrow[:, (2 * i + k) * 512:(2 * i + k + 1) * 512], start=True, stop=True)
+
+        def bias_co(i, eng):
+            dst = bias_bc[:, 2 * i:2 * i + 2, :].rearrange("p c n -> p (c n)")
+            if eng == "S":
+                nc.scalar.copy(out=dst, in_=bias_ps[i][:])
+            else:
+                nc.vector.tensor_copy(out=dst, in_=bias_ps[i][:])
+
+        order = [("X", 0), ("W", 0), ("H", 0), ("R", 0)]
+        for c in range(1, NCH):
+            order += [("W", c), ("R", c)]
+            if c == cfg["cx_after"]:
+                order.append(("cx", 0))
+
+        def next_load():
+            if st["load"] < len(order):
+                u = order[st["load"]]
+                st["load"] += 1
+                if u[0] == "cx":
+                    load_cx()
+                    next_load()
+                else:
+                    load_unit(u)
+
+        load_bias()
+        for k in range(cfg["nru"]):
+            next_load()
+
+        def head_unit(u, second=("V", "V"), do_quant=True):
+            for pr in (0, 1):
+                fills_pair(u, pr)
+                co(u, pr, "S")
+                co(u, 2 + pr, second[pr])
+            next_load()
+            if do_quant:
+                quant(u, 0)
+                quant(u, 1)
+
+        def mx_chunk_bt(c, bt, ss=(0, 1)):
+            for s in ss:
+                for g in range(2):
+                    mx(c, bt, s, g)
+
+        head_unit(("X", 0))
+        bias_mm(0, "gb0")
+        bias_mm(1, "gb1")
+        bias_co(0, "S")
+        bias_co(1, "S")
+        head_unit(("W", 0))
+        bias_mm(2, "gb2")
+        bias_mm(3, "tb4")
+        bias_co(2, "S")
+        bias_co(3, "S")
+        head_unit(("H", 0), second=("S", "V"))
+        for g in range(2):
+            for bt in range(4):
+                mx(0, bt, 0, g, "tb4" if bt == 3 else None)
+        head_unit(("R", 0), second=("S", "V"))
+        head_unit(("W", 1), second=("S", "S"), do_quant=False)
+        for bt in range(4):
+            mx_chunk_bt(0, bt, (1,))
+        quant(("W", 1), None)
+        for bt in range(4):
+            ba(0, bt)
+        st["ring"] = 5
+        head_unit(("R", 1), second=("S", "V"))
+        head_unit(("W", 2), second=("S", "S"), do_quant=False)
+        act1(0, ALL)
+        for bt in range(4):
+            mx_chunk_bt(1, bt)
+            if bt == 0:
+                quant(("W", 2), None)
+            ba(1, bt)
+        for i in range(4):
+            fill(("R", 2), i)
+        next_load()
+        for i in range(4):
+            co(("R", 2), i, "S")
+        quant(("R", 2), None)
+
+        for c in range(2, NCH - 1):
+            us = (("W", c + 1), ("R", c + 1))
+
+            def fill_i(i):
+                fill(us[i // 4], i % 4)
+                if i % 4 == 3:
+                    next_load()
+
+            def co_i(i):
+                co(us[i // 4], i % 4, "V" if i in cfg["vshare"] else "S")
+
+            if c >= 3:
+                ba(c - 1, 3)
+                op_ht(c - 3, ALL)
+                if c % 2 == 0:
+                    store(c - 4, c - 2, ALL)
+            for i in range(5):
+                fill_i(i)
+            for i in range(3):
+                co_i(i)
+                fill_i(5 + i)
+            co_i(3)
+            op_b(c - 2, ALL)
+            op_a(c - 2, ALL)
+            op_ct(c - 2, ALL)
+            quant(us[0], None)
+            for i in range(4, 8):
+                co_i(i)
+            act2(c - 2, ALL)
+            act1(c - 1, ALL)
+            for bt in range(4):
+                mx_chunk_bt(c, bt)
+                if bt < 3:
+                    ba(c, bt)
+                if bt == 0:
+                    quant(us[1], None)
+
+        c = NCH - 1
+        ba(c - 1, 3)
+        act1(c - 1, ALL)
+        op_ht(c - 3, ALL)
+        op_b(c - 2, ALL)
+        op_a(c - 2, ALL)
+        op_ct(c - 2, ALL)
+        act2(c - 2, ALL)
+        mx_chunk_bt(c, 0)
+        ba(c, 0)
+        op_b(c - 1, ALL)
+        op_a(c - 1, ALL)
+        mx_chunk_bt(c, 1)
+        ba(c, 1)
+        op_ct(c - 1, ALL)
+        act2(c - 1, ALL)
+        op_ht(c - 2, ALL)
+        store(4, 6, ALL)
+        act1(c, (0, 1))
+        mx_chunk_bt(c, 2)
+        ba(c, 2)
+        op_ht(c - 1, ALL)
+        store(6, 7, ALL)
+        op_b(c, (0, 1))
+        op_a(c, (0, 1))
+        op_ct(c, (0, 1))
+        act2(c, (0, 1))
+        mx_chunk_bt(c, 3)
+        act1(c, (2,))
+        ba(c, 3)
+        op_ht(c, (0, 1))
+        store(7, 8, (0, 1))
+        act1(c, (3,))
+        op_b(c, (2, 3))
+        op_a(c, (2, 3))
+        op_ct(c, (2, 3))
+        act2(c, (2, 3))
+        op_ht(c, (2, 3))
+        store(7, 8, (2, 3))

@@ -18,7 +18,8 @@ NCH = H // P
 ALL = (0, 1, 2, 3)
 FLOPS = 2 * B * (4 * H) * (I + H)
 
-CFG = {"cx_after": 3, "nru": 7, "vshare": (), "g_ops": (), "pin": True}
+G_OPS = tuple((name, c) for name in ("a", "b", "ct", "ht") for c in range(5))
+CFG = {"cx_after": 3, "nru": 7, "vshare": (1, 5), "g_ops": G_OPS, "pin": True}
 
 
 def tile_lstmcell_kernel(tc, xt, cx, hx, w_fg, w_ig, w_og, w_ci, r_fg, r_ig, r_og, r_ci,
@@ -315,8 +316,8 @@ def tile_lstmcell_kernel(tc, xt, cx, hx, w_fg, w_ig, w_og, w_ci, r_fg, r_ig, r_o
             quant(us[0], None)
             for i in range(4, 8):
                 co_i(i)
-            act2(c - 2, ALL)
             act1(c - 1, ALL)
+            act2(c - 2, ALL)
             for bt in range(4):
                 mx_chunk_bt(c, bt)
                 if bt < 3:

@@ -52,12 +52,13 @@ def tile_lstmcell_kernel(tc, xt, cx, hx, w_fg, w_ig, w_og, w_ci, r_fg, r_ig, r_o
         cx_sb = const.tile([P, 4, H], BF16, name="cx_sb")
         ct_all = const.tile([P, 4, H], F32, name="ct_all")
         ht_all = const.tile([P, 4, H], F32, name="ht_all")
+        wz = const.tile([P, 512], BF16, name="wz")
         warm = const.tile([P, 1], F32, name="warm")
         warm2 = const.tile([P, 1], F32, name="warm2")
         a_codes = [const.tile([P, 2, 512], U32, name="a_codes%d" % s, align_bytes=64) for s in range(2)]
         a_scales = [const.tile([P, 2, 512], U8, name="a_scales%d" % s, align_bytes=64) for s in range(2)]
 
-        st = {"fill": 0, "ring": 4, "g": 0, "load": 0}
+        st = {"fill": 0, "ring": 4, "g": 0, "load": 0, "dummy": 0}
         raws = {}
         banks = {}
         grps = {}
@@ -66,9 +67,10 @@ def tile_lstmcell_kernel(tc, xt, cx, hx, w_fg, w_ig, w_og, w_ci, r_fg, r_ig, r_o
         pres = {}
 
         def load_bias():
+            nc.vector.memset(wz[:].bitcast(I32), 0)
+            nc.vector.memset(ones[:], 1.0)
             nc.vector.memset(zrow[:].bitcast(I32), 0)
             nc.vector.memset(warm[:], 0.0)
-            nc.vector.memset(ones[:], 1.0)
             make_identity(nc, ident[:])
             zv = zrow[0:1, :].rearrange("o (c q h) -> o c q h", c=NCH, q=4)
             for q in range(4):
@@ -236,11 +238,23 @@ def tile_lstmcell_kernel(tc, xt, cx, hx, w_fg, w_ig, w_og, w_ci, r_fg, r_ig, r_o
         for k in range(cfg["nru"]):
             next_load()
 
-        def head_unit(u, second=("V", "V"), do_quant=True):
+        def dummy(n):
+            st["dummy"] += 1
+            dps = psum.tile([P, 512], F32, name="dummy%d" % st["dummy"], tag="tb4")
+            for k in range(n):
+                nc.tensor.matmul(out=dps[:], lhsT=ones[:], rhs=wz[:], start=True, stop=True)
+
+        def head_unit(u, second=("V", "V"), do_quant=True, bias=(None, None)):
             for pr in (0, 1):
                 fills_pair(u, pr)
+                if bias[pr] == "dummy":
+                    dummy(2)
+                elif bias[pr] is not None:
+                    bias_mm(bias[pr][0], bias[pr][1])
                 co(u, pr, "S")
                 co(u, 2 + pr, second[pr])
+                if bias[pr] is not None and bias[pr] != "dummy":
+                    bias_co(bias[pr][0], "S")
             next_load()
             if do_quant:
                 quant(u, 0)
@@ -251,17 +265,10 @@ def tile_lstmcell_kernel(tc, xt, cx, hx, w_fg, w_ig, w_og, w_ci, r_fg, r_ig, r_o
                 for g in range(2):
                     mx(c, bt, s, g)
 
-        head_unit(("X", 0))
-        bias_mm(0, "gb0")
-        bias_mm(1, "gb1")
-        bias_co(0, "S")
-        bias_co(1, "S")
-        head_unit(("W", 0))
-        bias_mm(2, "gb2")
-        bias_mm(3, "tb4")
-        bias_co(2, "S")
-        bias_co(3, "S")
-        head_unit(("H", 0), second=("S", "V"))
+        dummy(4)
+        head_unit(("X", 0), bias=("dummy", (0, "gb0")))
+        head_unit(("W", 0), bias=((1, "gb1"), (2, "gb2")))
+        head_unit(("H", 0), second=("S", "V"), bias=((3, "tb4"), None))
         for g in range(2):
             for bt in range(4):
                 mx(0, bt, 0, g, "tb4" if bt == 3 else None)

from contextlib import ExitStack

import concourse.mybir as mybir
from concourse.masks import make_identity

F32 = mybir.dt.float32
BF16 = mybir.dt.bfloat16
U32 = mybir.dt.uint32
U8 = mybir.dt.uint8
I32 = mybir.dt.int32
FP8X4 = mybir.dt.float8_e4m3fn_x4
ACT = mybir.ActivationFunctionType
ALU = mybir.AluOpType

P = 128
B, I, H = 512, 1024, 1024
NCH = H // P
ALL = (0, 1, 2, 3)
FLOPS = 2 * B * (4 * H) * (I + H)

G_OPS = tuple((name, c) for name in ("a", "b", "ct", "ht") for c in range(5))
CFG = {"cx_after": 3, "nru": 7, "vshare": (1, 5), "g_ops": G_OPS, "pin": True}


def tile_lstmcell_kernel(tc, xt, cx, hx, w_fg, w_ig, w_og, w_ci, r_fg, r_ig, r_og, r_ci,
                                    b_fg, b_ig, b_og, b_ci, out_0, out_1):
    nc = tc.nc
    cfg = CFG
    with ExitStack() as ctx:
        if cfg["pin"]:
            ctx.enter_context(tc.manual_schedule())
        const = ctx.enter_context(tc.tile_pool(name="const", bufs=1))
        raw_pool = ctx.enter_context(tc.tile_pool(name="raw", bufs=4 * cfg["nru"]))
        grp_pool = ctx.enter_context(tc.tile_pool(name="grp", bufs=3))
        wc_pool = ctx.enter_context(tc.tile_pool(name="wc", bufs=4))
        pre_pool = ctx.enter_context(tc.tile_pool(name="pre", bufs=4))
        psum = ctx.enter_context(tc.psum_pool(name="ps", bufs=1))

        w_in = (w_fg, w_ig, w_og, w_ci)
        r_in = (r_fg, r_ig, r_og, r_ci)
        b_in = (b_fg, b_ig, b_og, b_ci)
        xt_v = xt.rearrange("(m j) k -> m j k", j=4)
        hx_v = hx.rearrange("(m j) k -> m j k", j=4)
        cx_v = cx.rearrange("(m j) h -> m j h", j=4)
        ht_v = out_0.rearrange("(m j) h -> m j h", j=4)
        ct_v = out_1.rearrange("(m j) h -> m j h", j=4)

        ident = const.tile([P, P], F32, name="ident")
        ones = const.tile([P, P], BF16, name="ones")
        zrow = const.tile([P, 4 * H], BF16, name="zrow")
        bias_bc = const.tile([P, NCH, 512], BF16, name="bias_bc")
        cx_sb = const.tile([P, 4, H], BF16, name="cx_sb")
        ct_all = const.tile([P, 4, H], F32, name="ct_all")
        ht_all = const.tile([P, 4, H], F32, name="ht_all")
        wz = const.tile([P, 512], BF16, name="wz")
        warm = const.tile([P, 1], F32, name="warm")
        warm2 = const.tile([P, 1], F32, name="warm2")
        a_codes = [const.tile([P, 2, 512], U32, name="a_codes%d" % s, align_bytes=64) for s in range(2)]
        a_scales = [const.tile([P, 2, 512], U8, name="a_scales%d" % s, align_bytes=64) for s in range(2)]

        st = {"fill": 0, "ring": 4, "g": 0, "load": 0, "dummy": 0}
        raws = {}
        banks = {}
        grps = {}
        codes = {("X", 0): (a_codes[0], a_scales[0]), ("H", 0): (a_codes[1], a_scales[1])}
        gates = {}
        pres = {}

        def load_bias():
            nc.vector.memset(wz[:].bitcast(I32), 0)
            nc.vector.memset(ones[:], 1.0)
            nc.vector.memset(zrow[:].bitcast(I32), 0)
            nc.vector.memset(warm[:], 0.0)
            make_identity(nc, ident[:])
            zv = zrow[0:1, :].rearrange("o (c q h) -> o c q h", c=NCH, q=4)
            for q in range(4):
                nc.scalar.dma_start(out=zv[:, :, q, :], in_=b_in[q].rearrange("(o c h) -> o c h", o=1, c=NCH))
            nc.scalar.activation(out=warm2[:], in_=warm[:], func=ACT.Sigmoid)

        def load_unit(u):
            kind, c = u
            tiles = []
            for q in range(4):
                t = raw_pool.tile([P, 1024], BF16, name="raw_%s%d_%d" % (kind, c, q), tag="raw")
                if kind == "X":
                    src = xt_v[:, q, :]
                elif kind == "H":
                    src = hx_v[:, q, :]
                elif kind == "W":
                    src = w_in[q][c * P:(c + 1) * P, :]
                else:
                    src = r_in[q][c * P:(c + 1) * P, :]
                nc.sync.dma_start(out=t[:], in_=src)
                tiles.append(t)
            raws[u] = tiles

        def load_cx():
            nc.sync.dma_start(out=cx_sb[:], in_=cx_v)

        def bank_for(u, i):
            if (u, i) not in banks:
                tag = "tb%d" % (st["fill"] % st["ring"])
                st["fill"] += 1
                banks[(u, i)] = psum.tile([P, 512], F32, name="tp_%s%d_%d" % (u[0], u[1], i), tag=tag)
            return banks[(u, i)]

        def tr(u, q, g, w, ps, slot):
            col = 256 * g + 128 * w
            nc.tensor.transpose(out=ps[:, slot * P:(slot + 1) * P], in_=raws[u][q][:].bitcast(F32)[:, col:col + P],
                                identity=ident[:])

        def fill(u, i):
            g, pr = divmod(i, 2)
            ps = bank_for(u, i)
            for t in range(2):
                for w in range(2):
                    tr(u, 2 * pr + t, g, w, ps, 2 * t + w)

        def fills_pair(u, pr):
            for t in range(2):
                for g in range(2):
                    ps = bank_for(u, 2 * g + pr)
                    for w in range(2):
                        tr(u, 2 * pr + t, g, w, ps, 2 * t + w)

        def co(u, i, eng):
            g, pr = divmod(i, 2)
            if u not in grps:
                grps[u] = grp_pool.tile([P, 2, 2048], BF16, name="grp_%s%d" % u, tag="grp", align_bytes=64)
            dst = grps[u][:, g, pr * 1024:(pr + 1) * 1024].bitcast(F32).rearrange("p (t r w) -> p t r w", t=2, w=2)
            src = banks[(u, i)][:].rearrange("p (t w r) -> p t r w", t=2, w=2)
            if eng == "S":
                nc.scalar.copy(out=dst, in_=src)
            else:
                nc.vector.tensor_copy(out=dst, in_=src)

        def quant(u, g):
            if u not in codes:
                codes[u] = (wc_pool.tile([P, 2, 512], U32, name="wc_%s%d" % u, tag="wc", align_bytes=64),
                            wc_pool.tile([P, 2, 512], U8, name="ws_%s%d" % u, tag="ws", align_bytes=64))
            cd, sc = codes[u]
            if g is None:
                nc.vector.quantize_mx(out=cd[:].rearrange("p g n -> p (g n)").bitcast(FP8X4),
                                      scales=sc[:].rearrange("p g n -> p (g n)"),
                                      in_=grps[u][:].rearrange("p g n -> p (g n)"))
            else:
                nc.vector.quantize_mx(out=cd[:, g, :].bitcast(FP8X4), scales=sc[:, g, :], in_=grps[u][:, g, :])

        def mx(c, bt, s, g, bank=None):
            if (c, bt) not in gates:
                if bank is None:
                    bank = "gb%d" % (st["g"] % 3)
                    st["g"] += 1
                gates[(c, bt)] = psum.tile([P, 512], F32, name="gate_%d_%d" % (c, bt), tag=bank)
            acd, asc = codes[("XH"[s], 0)]
            wcd, wsc = codes[("WR"[s], c)]
            nc.tensor.matmul_mx(out=gates[(c, bt)][:],
                                lhsT=acd[:, g, bt * P:(bt + 1) * P].bitcast(FP8X4),
                                lhsT_scale=asc[:, g, bt * P:(bt + 1) * P],
                                rhs=wcd[:, g, :].bitcast(FP8X4),
                                rhs_scale=wsc[:, g, :],
                                start=(s == 0 and g == 0), stop=(s == 1 and g == 1))

        def ba(c, bt):
            if c not in pres:
                pres[c] = pre_pool.tile([P, 4, 512], F32, name="pre_%d" % c, tag="pre")
            nc.vector.tensor_tensor(out=pres[c][:, bt, :], in0=gates[(c, bt)][:], in1=bias_bc[:, c, :], op=ALU.add)

        def act1(c, bts):
            b0, b1 = bts[0], bts[-1] + 1
            nc.scalar.activation(out=pres[c][:, b0:b1, 0:384], in_=pres[c][:, b0:b1, 0:384], func=ACT.Sigmoid)
            nc.scalar.activation(out=pres[c][:, b0:b1, 384:512], in_=pres[c][:, b0:b1, 384:512], func=ACT.Tanh)

        def ew_eng(name, c):
            return nc.gpsimd if (name, c) in cfg["g_ops"] else nc.vector

        def op_a(c, bts):
            b0, b1 = bts[0], bts[-1] + 1
            ew_eng("a", c).tensor_tensor(out=pres[c][:, b0:b1, 0:128], in0=pres[c][:, b0:b1, 0:128],
                                         in1=cx_sb[:, b0:b1, c * P:(c + 1) * P], op=ALU.mult)

        def op_b(c, bts):
            b0, b1 = bts[0], bts[-1] + 1
            ew_eng("b", c).tensor_tensor(out=pres[c][:, b0:b1, 128:256], in0=pres[c][:, b0:b1, 128:256],
                                         in1=pres[c][:, b0:b1, 384:512], op=ALU.mult)

        def op_ct(c, bts):
            b0, b1 = bts[0], bts[-1] + 1
            ew_eng("ct", c).tensor_tensor(out=ct_all[:, b0:b1, c * P:(c + 1) * P], in0=pres[c][:, b0:b1, 0:128],
                                          in1=pres[c][:, b0:b1, 128:256], op=ALU.add)

        def act2(c, bts):
            b0, b1 = bts[0], bts[-1] + 1
            nc.scalar.activation(out=pres[c][:, b0:b1, 384:512], in_=ct_all[:, b0:b1, c * P:(c + 1) * P], func=ACT.Tanh)

        def op_ht(c, bts):
            b0, b1 = bts[0], bts[-1] + 1
            ew_eng("ht", c).tensor_tensor(out=ht_all[:, b0:b1, c * P:(c + 1) * P], in0=pres[c][:, b0:b1, 256:384],
                                          in1=pres[c][:, b0:b1, 384:512], op=ALU.mult)

        def store(c0, c1, bts):
            b0, b1 = bts[0], bts[-1] + 1
            nc.sync.dma_start(out=ct_v[:, b0:b1, c0 * P:c1 * P], in_=ct_all[:, b0:b1, c0 * P:c1 * P])
            nc.sync.dma_start(out=ht_v[:, b0:b1, c0 * P:c1 * P], in_=ht_all[:, b0:b1, c0 * P:c1 * P])

        bias_ps = {}

        def bias_mm(i, bank):
            bias_ps[i] = psum.tile([P, 1024], BF16, name="bias_ps%d" % i, tag=bank)
            for k in range(2):
                nc.tensor.matmul(out=bias_ps[i][:, k * 512:(k + 1) * 512], lhsT=ones[:],
                                 rhs=zrow[:, (2 * i + k) * 512:(2 * i + k + 1) * 512], start=True, stop=True)

        def bias_co(i, eng):
            dst = bias_bc[:, 2 * i:2 * i + 2, :].rearrange("p c n -> p (c n)")
            if eng == "S":
                nc.scalar.copy(out=dst, in_=bias_ps[i][:])
            else:
                nc.vector.tensor_copy(out=dst, in_=bias_ps[i][:])

        order = [("X", 0), ("W", 0), ("H", 0), ("R", 0)]
        for c in range(1, NCH):
            order += [("W", c), ("R", c)]
            if c == cfg["cx_after"]:
                order.append(("cx", 0))

        def next_load():
            if st["load"] < len(order):
                u = order[st["load"]]
                st["load"] += 1
                if u[0] == "cx":
                    load_cx()
                    next_load()
                else:
                    load_unit(u)

        load_bias()
        for k in range(cfg["nru"]):
            next_load()

        def dummy(n):
            st["dummy"] += 1
            dps = psum.tile([P, 512], F32, name="dummy%d" % st["dummy"], tag="tb4")
            for k in range(n):
                nc.tensor.matmul(out=dps[:], lhsT=ones[:], rhs=wz[:], start=True, stop=True)

        def head_unit(u, second=("V", "V"), do_quant=True, bias=(None, None)):
            for pr in (0, 1):
                fills_pair(u, pr)
                if bias[pr] == "dummy":
                    dummy(2)
                elif bias[pr] is not None:
                    bias_mm(bias[pr][0], bias[pr][1])
                co(u, pr, "S")
                co(u, 2 + pr, second[pr])
                if bias[pr] is not None and bias[pr] != "dummy":
                    bias_co(bias[pr][0], "S")
            next_load()
            if do_quant:
                quant(u, 0)
                quant(u, 1)

        def mx_chunk_bt(c, bt, ss=(0, 1)):
            for s in ss:
                for g in range(2):
                    mx(c, bt, s, g)

        dummy(4)
        head_unit(("X", 0), bias=("dummy", (0, "gb0")))
        head_unit(("W", 0), bias=((1, "gb1"), (2, "gb2")))
        head_unit(("H", 0), second=("S", "V"), bias=((3, "tb4"), None))
        for g in range(2):
            for bt in range(4):
                mx(0, bt, 0, g, "tb4" if bt == 3 else None)
        head_unit(("R", 0), second=("S", "V"))
        head_unit(("W", 1), second=("S", "S"), do_quant=False)
        for bt in range(4):
            mx_chunk_bt(0, bt, (1,))
        quant(("W", 1), None)
        for bt in range(4):
            ba(0, bt)
        st["ring"] = 5
        head_unit(("R", 1), second=("S", "V"))
        head_unit(("W", 2), second=("S", "S"), do_quant=False)
        act1(0, ALL)
        for bt in range(4):
            mx_chunk_bt(1, bt)
            if bt == 0:
                quant(("W", 2), None)
            ba(1, bt)
        for i in range(4):
            fill(("R", 2), i)
        next_load()
        for i in range(4):
            co(("R", 2), i, "S")
        quant(("R", 2), None)

        for c in range(2, NCH - 1):
            us = (("W", c + 1), ("R", c + 1))

            def fill_i(i):
                fill(us[i // 4], i % 4)
                if i % 4 == 3:
                    next_load()

            def co_i(i):
                co(us[i // 4], i % 4, "V" if i in cfg["vshare"] else "S")

            if c >= 3:
                ba(c - 1, 3)
                op_ht(c - 3, ALL)
                if c % 2 == 0:
                    store(c - 4, c - 2, ALL)
            for i in range(5):
                fill_i(i)
            for i in range(3):
                co_i(i)
                fill_i(5 + i)
            co_i(3)
            op_b(c - 2, ALL)
            op_a(c - 2, ALL)
            op_ct(c - 2, ALL)
            quant(us[0], None)
            for i in range(4, 8):
                co_i(i)
            act1(c - 1, ALL)
            act2(c - 2, ALL)
            for bt in range(4):
                mx_chunk_bt(c, bt)
                if bt < 3:
                    ba(c, bt)
                if bt == 0:
                    quant(us[1], None)

        c = NCH - 1
        ba(c - 1, 3)
        act1(c - 1, ALL)
        op_ht(c - 3, ALL)
        op_b(c - 2, ALL)
        op_a(c - 2, ALL)
        op_ct(c - 2, ALL)
        act2(c - 2, ALL)
        mx_chunk_bt(c, 0)
        ba(c, 0)
        op_b(c - 1, ALL)
        op_a(c - 1, ALL)
        mx_chunk_bt(c, 1)
        ba(c, 1)
        op_ct(c - 1, ALL)
        act2(c - 1, ALL)
        op_ht(c - 2, ALL)
        store(4, 6, ALL)
        act1(c, (0, 1))
        mx_chunk_bt(c, 2)
        ba(c, 2)
        op_ht(c - 1, ALL)
        store(6, 7, ALL)
        op_b(c, (0, 1))
        op_a(c, (0, 1))
        op_ct(c, (0, 1))
        act2(c, (0, 1))
        mx_chunk_bt(c, 3)
        act1(c, (2,))
        ba(c, 3)
        op_ht(c, (0, 1))
        store(7, 8, (0, 1))
        act1(c, (3,))
        op_b(c, (2, 3))
        op_a(c, (2, 3))
        op_ct(c, (2, 3))
        act2(c, (2, 3))
        op_ht(c, (2, 3))
        store(7, 8, (2, 3))
